import numpy as np
import ml_dtypes


def mxq(x, axis, fmt="e4m3"):
    dtype, down = {"e4m3": (ml_dtypes.float8_e4m3fn, 7), "e5m2": (ml_dtypes.float8_e5m2, 14)}[fmt]
    v = np.moveaxis(np.asarray(x, np.float32).astype(ml_dtypes.bfloat16).astype(np.float64), axis, -1)
    blocks = v.reshape(v.shape[:-1] + (-1, 32))
    amax = np.abs(blocks).max(-1, keepdims=True)
    byte = np.maximum(np.where(amax > 0, np.frexp(amax)[1] - 1 + 127, 0) - down, 1)
    scale = np.exp2(byte - 127.0)
    codes = (blocks / scale).astype(np.float32).astype(dtype).astype(np.float64)
    return np.moveaxis((codes * scale).reshape(v.shape), -1, axis)


WIDE = False


def mx_kscale(k):
    if not WIDE:
        return np.ones(k)
    levels = np.array([10, -10, 5, -5, 0])
    a = np.random.permutation(np.resize(levels, k // 512 * 4)).reshape(k // 512, 4)
    idx = np.arange(k)
    return np.exp2(a[idx // 512, idx % 128 // 32])


BF16 = ml_dtypes.bfloat16


def bf(x):
    return np.asarray(x, np.float32).astype(BF16)


def f64(x):
    return np.asarray(x).astype(np.float64)


B, P, WS, D, H = 2, 64, 8, 512, 8
WN = P // WS
N = WS * WS
SHIFT = WS // 2
LN_EPS = 1e-5


def layer_norm(x, g, b):
    mu = x.mean(-1, keepdims=True)
    var = x.var(-1, keepdims=True)
    return (x - mu) / np.sqrt(var + LN_EPS) * g + b


def window_merge(win):
    x = win.reshape(B, WN, WN, WS, WS, D).transpose(0, 1, 3, 2, 4, 5)
    return x.reshape(B, P, P, D)


def setup_inputs():
    s, t = mx_kscale(D), mx_kscale(D)
    x_mid = np.random.standard_normal((B, P * P, D)) * 1.4 + np.random.standard_normal((B, P * P, 1)) * 0.5
    return {"attn_win": bf(np.random.standard_normal((B * WN * WN, N, D)) * 0.4 * s),
            "x_mid": bf(x_mid),
            "Wo2": bf(np.random.standard_normal((D, D)) / np.sqrt(D) / s[:, None]),
            "bo2": bf(0.1 * np.random.standard_normal(D)),
            "g4": bf((1.0 + 0.1 * np.random.standard_normal(D)) * t),
            "b4": bf(0.1 * np.random.standard_normal(D) * t),
            "Wl": bf(np.random.standard_normal((D, D)) / np.sqrt(D) / t[:, None]),
            "bl": bf(0.1 * np.random.standard_normal(D))}


def reference(attn_win, x_mid, Wo2, bo2, g4, b4, Wl, bl):
    a = (mxq(f64(attn_win), 2, "e4m3") @ mxq(f64(Wo2), 0, "e4m3")) + f64(bo2)
    a = np.roll(window_merge(a), (-SHIFT, -SHIFT), axis=(1, 2)).reshape(B, P * P, D)
    x = f64(x_mid) + a
    h = layer_norm(x, f64(g4), f64(b4))
    return x + (mxq(h, 2, "e4m3") @ mxq(f64(Wl), 0, "e4m3")) + f64(bl)

@@ -1,0 +1,332 @@
+from contextlib import ExitStack
+
+import concourse.mybir as mybir
+from concourse.masks import make_identity
+
+F32 = mybir.dt.float32
+BF16 = mybir.dt.bfloat16
+U32 = mybir.dt.uint32
+U8 = mybir.dt.uint8
+FP8X4 = mybir.dt.float8_e4m3fn_x4
+ADD = mybir.AluOpType.add
+MULT = mybir.AluOpType.mult
+ACT = mybir.ActivationFunctionType
+
+P = 128
+D = 512
+PACK = 4
+QUAD = 4
+GROUP = P * QUAD
+IMAGES = 2
+WINDOW_ROWS = 8
+WS = 8
+GROUPS = IMAGES * WINDOW_ROWS
+IMAGE_TOKENS = WINDOW_ROWS * GROUP
+ROW_QUADS = 16
+SHIFT_TOKENS = GROUP // 2
+LN_EPS = 1e-5
+
+FLOPS = 2 * 2 * IMAGES * IMAGE_TOKENS * D * D
+
+
+def quads(flat, first, count):
+    return flat[first : first + count, :].rearrange("(p q) d -> p q d", q=QUAD)
+
+
+def image_pieces(g):
+    image, window_row = divmod(g, WINDOW_ROWS)
+    base = image * IMAGE_TOKENS
+    if window_row == 0:
+        half = P // 2
+        return [(0, half, base + IMAGE_TOKENS - SHIFT_TOKENS), (half, half, base)]
+    return [(0, P, base + window_row * GROUP - SHIFT_TOKENS)]
+
+
+def quantise_weight(nc, stage, keep, raw, label):
+    grouped = stage.tile([P, D, PACK], BF16, name="grouped_" + label, align_bytes=64)
+    nc.vector.tensor_copy(out=grouped[:], in_=raw[:].rearrange("p t n -> p n t"))
+    codes = keep.tile([P, D], U32, name="codes_" + label, align_bytes=64)
+    scales = keep.tile([P, D], U8, name="scales_" + label, align_bytes=64)
+    nc.vector.quantize_mx(
+        out=codes[:].bitcast(FP8X4), scales=scales[:], in_=grouped[:].rearrange("p n t -> p (n t)")
+    )
+    return codes, scales
+
+
+def tile_successiveswintransfomerblock_pb_t_kernel(tc, attn_win, x_mid, Wo2, bo2, g4, b4, Wl, bl, out):
+    nc = tc.nc
+    attn_flat = attn_win.flatten_outer_dims()
+    x_flat = x_mid.flatten_outer_dims()
+    out_flat = out.flatten_outer_dims()
+
+    with ExitStack() as ctx:
+        keep = ctx.enter_context(tc.tile_pool(name="keep", bufs=1))
+        stage = ctx.enter_context(tc.tile_pool(name="stage", bufs=1))
+        loads = ctx.enter_context(tc.tile_pool(name="loads", bufs=3))
+        work = ctx.enter_context(tc.tile_pool(name="work", bufs=2))
+        resid = ctx.enter_context(tc.tile_pool(name="resid", bufs=6))
+        stats = ctx.enter_context(tc.tile_pool(name="stats", bufs=4))
+        psum_at = ctx.enter_context(tc.psum_pool(name="psum_at", bufs=2))
+        psum_mm = ctx.enter_context(tc.psum_pool(name="psum_mm", bufs=4))
+        psum_zt = ctx.enter_context(tc.psum_pool(name="psum_zt", bufs=2))
+        ctx.enter_context(tc.manual_schedule())
+
+        gb_rows = keep.tile([P, P], BF16, name="gb_rows")
+        nc.vector.memset(gb_rows[:], 0.0)
+        eps_col = keep.tile([P, 1], F32, name="eps_col")
+        nc.vector.memset(eps_col[:], LN_EPS)
+
+        wo_raw = stage.tile([P, PACK, D], BF16, name="wo_raw")
+        for u in range(2):
+            nc.sync.dma_start(
+                out=wo_raw[:, 2 * u : 2 * u + 2, :],
+                in_=Wo2[u * 2 * P : (u + 1) * 2 * P, :].rearrange("(p e) n -> p e n", e=2),
+            )
+        wl_raw = stage.tile([P, PACK, D], BF16, name="wl_raw")
+        nc.sync.dma_start(out=wl_raw[:], in_=Wl.rearrange("(t p) n -> p t n", p=P))
+        nc.scalar.dma_start(out=gb_rows[0:PACK, :], in_=g4.rearrange("(t p) -> t p", p=P))
+        nc.scalar.dma_start(out=gb_rows[PACK : 2 * PACK, :], in_=b4.rearrange("(t p) -> t p", p=P))
+        bo2_all = keep.tile([P, D], BF16, name="bo2_all")
+        nc.scalar.dma_start(out=bo2_all[:], in_=bo2.partition_broadcast(P))
+        bl_all = keep.tile([P, D], BF16, name="bl_all")
+        nc.scalar.dma_start(out=bl_all[:], in_=bl.partition_broadcast(P))
+
+        ident = keep.tile([P, P], F32, name="ident")
+        make_identity(nc, ident[:])
+        by_row = keep.tile([P, P], F32, name="by_row")
+        nc.vector.tensor_copy(
+            out=by_row[:].rearrange("p (r w h) -> p r w h", r=WS, w=WS),
+            in_=ident[:].rearrange("p (w r h) -> p r w h", w=WS, r=WS),
+        )
+        to_image = keep.tile([P, P], F32, name="to_image")
+        unrolled = by_row[:].rearrange("p (r m) -> p r m", m=ROW_QUADS)
+        rolled = to_image[:].rearrange("p (r m) -> p r m", m=ROW_QUADS)
+        nc.vector.tensor_copy(out=rolled[:, :, 0 : ROW_QUADS - 1], in_=unrolled[:, :, 1:ROW_QUADS])
+        nc.vector.tensor_copy(out=rolled[:, :, ROW_QUADS - 1 : ROW_QUADS], in_=unrolled[:, :, 0:1])
+        ident_bf = keep.tile([P, P], BF16, name="ident_bf")
+        nc.vector.tensor_copy(out=ident_bf[:], in_=ident[:])
+
+        wo_codes, wo_scales = quantise_weight(nc, stage, keep, wo_raw, "wo")
+        wl_codes, wl_scales = quantise_weight(nc, stage, keep, wl_raw, "wl")
+
+        gb_ps = psum_mm.tile([P, P], BF16, name="gb_ps", tag="acc")
+        nc.tensor.transpose(gb_ps[:], gb_rows[:], ident_bf[:])
+        gb_col = keep.tile([P, 2 * PACK], F32, name="gb_col")
+        nc.vector.tensor_copy(out=gb_col[:], in_=gb_ps[:, 0 : 2 * PACK])
+
+        live = {}
+
+        def load(g):
+            if not 0 <= g < GROUPS:
+                return
+            attn_sb = loads.tile([P, QUAD, D], BF16, name="attn_sb")
+            nc.sync.dma_start(out=attn_sb[:], in_=quads(attn_flat, g * GROUP, GROUP))
+            xm_sb = loads.tile([P, QUAD, D], BF16, name="xm_sb")
+            for first_p, n_p, first_token in image_pieces(g):
+                nc.sync.dma_start(out=xm_sb[first_p : first_p + n_p], in_=quads(x_flat, first_token, n_p * QUAD))
+            live["attn_sb", g] = attn_sb
+            live["xm_sb", g] = xm_sb
+
+        def attn_transpose(g):
+            if not 0 <= g < GROUPS:
+                return
+            attn_words = live["attn_sb", g][:].bitcast(F32)
+            for pair in range(QUAD // 2):
+                a_t = psum_at.tile([P, 2, 2, P], F32, name="a_t")
+                for s in range(2):
+                    for u in range(2):
+                        nc.tensor.transpose(
+                            a_t[:, s, u, :], attn_words[:, 2 * pair + s, u * P : (u + 1) * P], to_image[:]
+                        )
+                live["a_t", g, pair] = a_t
+
+        def attn_copy_out(g):
+            if not 0 <= g < GROUPS:
+                return
+            a_grouped = work.tile([P, QUAD, P, PACK], BF16, name="a_grouped", align_bytes=64)
+            for pair in range(QUAD // 2):
+                nc.scalar.copy(
+                    out=a_grouped[:, 2 * pair : 2 * pair + 2].bitcast(F32),
+                    in_=live["a_t", g, pair][:].rearrange("p s u r -> p s r u"),
+                )
+            live["a_grouped", g] = a_grouped
+
+        def quantise_attn(g):
+            if not 0 <= g < GROUPS:
+                return
+            a_codes = work.tile([P, GROUP], U32, name="a_codes", align_bytes=64)
+            a_scales = work.tile([P, GROUP], U8, name="a_scales", align_bytes=64)
+            nc.vector.quantize_mx(
+                out=a_codes[:].bitcast(FP8X4),
+                scales=a_scales[:],
+                in_=live["a_grouped", g][:].rearrange("p q r t -> p (q r t)"),
+            )
+            live["a_codes", g] = a_codes
+            live["a_scales", g] = a_scales
+
+        def add_bo2(g):
+            if not 0 <= g < GROUPS:
+                return
+            x = resid.tile([P, QUAD, D], F32, name="x")
+            nc.vector.tensor_tensor(
+                out=x[:], in0=live["xm_sb", g][:], in1=bo2_all[:].unsqueeze(1).to_broadcast([P, QUAD, D]), op=ADD
+            )
+            live["x", g] = x
+
+        def first_product(g):
+            if not 0 <= g < GROUPS:
+                return
+            x = live["x", g]
+            x_sum = stats.tile([P, QUAD], F32, name="x_sum")
+            for q in range(QUAD):
+                tokens = slice(q * P, (q + 1) * P)
+                acc1 = psum_mm.tile([P, D], F32, name="acc1", tag="acc")
+                nc.tensor.matmul_mx(
+                    out=acc1[:],
+                    lhsT=live["a_codes", g][:, tokens].bitcast(FP8X4),
+                    lhsT_scale=live["a_scales", g][:, tokens],
+                    rhs=wo_codes[:].bitcast(FP8X4),
+                    rhs_scale=wo_scales[:],
+                    start=True,
+                    stop=True,
+                )
+                nc.vector.scalar_tensor_tensor(
+                    out=x[:, q, :],
+                    in0=acc1[:],
+                    scalar=1.0,
+                    in1=x[:, q, :],
+                    op0=MULT,
+                    op1=ADD,
+                    accum_out=x_sum[:, q : q + 1],
+                )
+            neg_mean = stats.tile([P, QUAD], F32, name="neg_mean")
+            nc.vector.tensor_scalar_mul(out=neg_mean[:], in0=x_sum[:], scalar1=-1.0 / D)
+            live["neg_mean", g] = neg_mean
+
+        def variance(g):
+            if not 0 <= g < GROUPS:
+                return
+            neg_mean = live["neg_mean", g]
+            sq_sum = stats.tile([P, QUAD], F32, name="sq_sum")
+            for q in range(QUAD):
+                squares = work.tile([P, D], BF16, name="squares")
+                nc.scalar.activation(
+                    out=squares[:],
+                    in_=live["x", g][:, q, :],
+                    func=ACT.Square,
+                    bias=neg_mean[:, q : q + 1],
+                    scale=1.0,
+                    accum_out=sq_sum[:, q : q + 1],
+                )
+            std = stats.tile([P, QUAD], F32, name="std")
+            nc.scalar.activation(out=std[:], in_=sq_sum[:], func=ACT.Sqrt, bias=eps_col[:], scale=1.0 / D)
+            rstd = stats.tile([P, QUAD], F32, name="rstd")
+            nc.vector.reciprocal(out=rstd[:], in_=std[:])
+            shift = stats.tile([P, QUAD], F32, name="shift")
+            nc.vector.tensor_tensor(out=shift[:], in0=neg_mean[:], in1=rstd[:], op=MULT)
+            live["rstd", g] = rstd
+            live["shift", g] = shift
+
+        def normalise(g):
+            if not 0 <= g < GROUPS:
+                return
+            z = work.tile([P, QUAD, D], F32, name="z")
+            for q in range(QUAD):
+                nc.scalar.activation(
+                    out=z[:, q, :],
+                    in_=live["x", g][:, q, :],
+                    func=ACT.Identity,
+                    bias=live["shift", g][:, q : q + 1],
+                    scale=live["rstd", g][:, q : q + 1],
+                )
+            live["z", g] = z
+
+        def z_transpose(g, t):
+            if not 0 <= g < GROUPS:
+                return
+            z_t = psum_zt.tile([P, GROUP], F32, name="z_t")
+            for q in range(QUAD):
+                nc.tensor.transpose(z_t[:, q * P : (q + 1) * P], live["z", g][:, q, t * P : (t + 1) * P], ident[:])
+            live["z_t", g, t] = z_t
+
+        def gain_and_bias(g, t):
+            if not 0 <= g < GROUPS:
+                return
+            if t == 0:
+                live["h_t", g] = work.tile([P, PACK, GROUP], BF16, name="h_t")
+            nc.scalar.activation(
+                out=live["h_t", g][:, t, :],
+                in_=live["z_t", g, t][:],
+                func=ACT.Identity,
+                bias=gb_col[:, PACK + t : PACK + t + 1],
+                scale=gb_col[:, t : t + 1],
+            )
+
+        def regroup_h(g):
+            if not 0 <= g < GROUPS:
+                return
+            h_grouped = work.tile([P, GROUP, PACK], BF16, name="h_grouped", align_bytes=64)
+            nc.scalar.copy(
+                out=h_grouped[:].rearrange("p (c i) t -> p c t i", i=4),
+                in_=live["h_t", g][:].rearrange("p t (c i) -> p c t i", i=4),
+            )
+            live["h_grouped", g] = h_grouped
+
+        def quantise_h(g):
+            if not 0 <= g < GROUPS:
+                return
+            h_codes = work.tile([P, GROUP], U32, name="h_codes", align_bytes=64)
+            h_scales = work.tile([P, GROUP], U8, name="h_scales", align_bytes=64)
+            nc.vector.quantize_mx(
+                out=h_codes[:].bitcast(FP8X4),
+                scales=h_scales[:],
+                in_=live["h_grouped", g][:].rearrange("p r t -> p (r t)"),
+            )
+            live["h_codes", g] = h_codes
+            live["h_scales", g] = h_scales
+
+        def add_bl(g):
+            if not 0 <= g < GROUPS:
+                return
+            x = live["x", g]
+            nc.vector.tensor_tensor(out=x[:], in0=x[:], in1=bl_all[:].unsqueeze(1).to_broadcast([P, QUAD, D]), op=ADD)
+
+        def second_product(g):
+            if not 0 <= g < GROUPS:
+                return
+            x = live["x", g]
+            for q in range(QUAD):
+                tokens = slice(q * P, (q + 1) * P)
+                acc2 = psum_mm.tile([P, D], F32, name="acc2", tag="acc")
+                nc.tensor.matmul_mx(
+                    out=acc2[:],
+                    lhsT=live["h_codes", g][:, tokens].bitcast(FP8X4),
+                    lhsT_scale=live["h_scales", g][:, tokens],
+                    rhs=wl_codes[:].bitcast(FP8X4),
+                    rhs_scale=wl_scales[:],
+                    start=True,
+                    stop=True,
+                )
+                nc.vector.tensor_tensor(out=x[:, q, :], in0=acc2[:], in1=x[:, q, :], op=ADD)
+            for first_p, n_p, first_token in image_pieces(g):
+                nc.sync.dma_start(out=quads(out_flat, first_token, n_p * QUAD), in_=x[first_p : first_p + n_p])
+
+        for step in range(-3, GROUPS + 2):
+            load(step + 3)
+            attn_transpose(step + 1)
+            quantise_h(step - 2)
+            add_bl(step - 1)
+            variance(step)
+            attn_copy_out(step + 1)
+            second_product(step - 2)
+            normalise(step)
+            quantise_attn(step + 1)
+            regroup_h(step - 1)
+            add_bo2(step + 2)
+            z_transpose(step, 0)
+            z_transpose(step, 1)
+            first_product(step + 1)
+            for t in range(PACK):
+                gain_and_bias(step, t)
+                if t + 2 < PACK:
+                    z_transpose(step, t + 2)

@@ -25,6 +25,7 @@ IMAGE_TOKENS = WINDOW_ROWS * GROUP
 ROW_QUADS = 16
 SHIFT_TOKENS = GROUP // 2
 LN_EPS = 1e-5
+Z_BANKS = 3
 
 FLOPS = 2 * 2 * IMAGES * IMAGE_TOKENS * D * D
 
@@ -67,8 +68,8 @@ def tile_successiveswintransfomerblock_pb_t_kernel(tc, attn_win, x_mid, Wo2, bo2
         resid = ctx.enter_context(tc.tile_pool(name="resid", bufs=6))
         stats = ctx.enter_context(tc.tile_pool(name="stats", bufs=4))
         psum_at = ctx.enter_context(tc.psum_pool(name="psum_at", bufs=2))
-        psum_mm = ctx.enter_context(tc.psum_pool(name="psum_mm", bufs=4))
-        psum_zt = ctx.enter_context(tc.psum_pool(name="psum_zt", bufs=2))
+        psum_mm = ctx.enter_context(tc.psum_pool(name="psum_mm", bufs=3))
+        psum_zt = ctx.enter_context(tc.psum_pool(name="psum_zt", bufs=Z_BANKS))
         ctx.enter_context(tc.manual_schedule())
 
         gb_rows = keep.tile([P, P], BF16, name="gb_rows")
@@ -143,7 +144,7 @@ def tile_successiveswintransfomerblock_pb_t_kernel(tc, attn_win, x_mid, Wo2, bo2
         def attn_copy_out(g):
             if not 0 <= g < GROUPS:
                 return
-            a_grouped = work.tile([P, QUAD, P, PACK], BF16, name="a_grouped", align_bytes=64)
+            a_grouped = work.tile([P, QUAD, P, PACK], BF16, name="a_grouped", bufs=3, align_bytes=64)
             for pair in range(QUAD // 2):
                 nc.scalar.copy(
                     out=a_grouped[:, 2 * pair : 2 * pair + 2].bitcast(F32),
@@ -308,25 +309,27 @@ def tile_successiveswintransfomerblock_pb_t_kernel(tc, attn_win, x_mid, Wo2, bo2
                     stop=True,
                 )
                 nc.vector.tensor_tensor(out=x[:, q, :], in0=acc2[:], in1=x[:, q, :], op=ADD)
-            for first_p, n_p, first_token in image_pieces(g):
-                nc.sync.dma_start(out=quads(out_flat, first_token, n_p * QUAD), in_=x[first_p : first_p + n_p])
+                for first_p, n_p, first_token in image_pieces(g):
+                    nc.sync.dma_start(
+                        out=quads(out_flat, first_token, n_p * QUAD)[:, q, :], in_=x[first_p : first_p + n_p, q, :]
+                    )
 
         for step in range(-3, GROUPS + 2):
             load(step + 3)
-            attn_transpose(step + 1)
+            attn_transpose(step + 2)
             quantise_h(step - 2)
             add_bl(step - 1)
             variance(step)
-            attn_copy_out(step + 1)
-            second_product(step - 2)
-            normalise(step)
             quantise_attn(step + 1)
-            regroup_h(step - 1)
-            add_bo2(step + 2)
-            z_transpose(step, 0)
-            z_transpose(step, 1)
+            attn_copy_out(step + 2)
+            second_product(step - 2)
             first_product(step + 1)
+            add_bo2(step + 2)
+            normalise(step)
+            regroup_h(step - 1)
+            for t in range(Z_BANKS):
+                z_transpose(step, t)
             for t in range(PACK):
                 gain_and_bias(step, t)
-                if t + 2 < PACK:
-                    z_transpose(step, t + 2)
+                if t + Z_BANKS < PACK:
+                    z_transpose(step, t + Z_BANKS)

@@ -201,7 +201,7 @@ def tile_successiveswintransfomerblock_pb_t_kernel(tc, attn_win, x_mid, Wo2, bo2
                     accum_out=x_sum[:, q : q + 1],
                 )
             neg_mean = stats.tile([P, QUAD], F32, name="neg_mean")
-            nc.vector.tensor_scalar_mul(out=neg_mean[:], in0=x_sum[:], scalar1=-1.0 / D)
+            nc.gpsimd.tensor_scalar(out=neg_mean[:], in0=x_sum[:], scalar1=-1.0 / D, scalar2=0.0, op0=MULT, op1=ADD)
             live["neg_mean", g] = neg_mean
 
         def variance(g):
@@ -219,12 +219,12 @@ def tile_successiveswintransfomerblock_pb_t_kernel(tc, attn_win, x_mid, Wo2, bo2
                     scale=1.0,
                     accum_out=sq_sum[:, q : q + 1],
                 )
-            std = stats.tile([P, QUAD], F32, name="std")
-            nc.scalar.activation(out=std[:], in_=sq_sum[:], func=ACT.Sqrt, bias=eps_col[:], scale=1.0 / D)
             rstd = stats.tile([P, QUAD], F32, name="rstd")
-            nc.vector.reciprocal(out=rstd[:], in_=std[:])
+            nc.scalar.activation(
+                out=rstd[:], in_=sq_sum[:], func=ACT.Abs_reciprocal_sqrt, bias=eps_col[:], scale=1.0 / D
+            )
             shift = stats.tile([P, QUAD], F32, name="shift")
-            nc.vector.tensor_tensor(out=shift[:], in0=neg_mean[:], in1=rstd[:], op=MULT)
+            nc.gpsimd.tensor_tensor(out=shift[:], in0=neg_mean[:], in1=rstd[:], op=MULT)
             live["rstd", g] = rstd
             live["shift", g] = shift
 

@@ -169,9 +169,8 @@ def tile_successiveswintransfomerblock_pb_t_kernel(tc, attn_win, x_mid, Wo2, bo2
             if not 0 <= g < GROUPS:
                 return
             x = resid.tile([P, QUAD, D], F32, name="x")
-            nc.vector.tensor_tensor(
-                out=x[:], in0=live["xm_sb", g][:], in1=bo2_all[:].unsqueeze(1).to_broadcast([P, QUAD, D]), op=ADD
-            )
+            for q in range(QUAD):
+                nc.gpsimd.tensor_tensor(out=x[:, q, :], in0=live["xm_sb", g][:, q, :], in1=bo2_all[:], op=ADD)
             live["x", g] = x
 
         def first_product(g):
@@ -320,11 +319,11 @@ def tile_successiveswintransfomerblock_pb_t_kernel(tc, attn_win, x_mid, Wo2, bo2
             quantise_h(step - 2)
             add_bl(step - 1)
             variance(step)
+            add_bo2(step + 2)
             quantise_attn(step + 1)
             attn_copy_out(step + 2)
             second_product(step - 2)
             first_product(step + 1)
-            add_bo2(step + 2)
             normalise(step)
             regroup_h(step - 1)
             for t in range(Z_BANKS):

@@ -25,6 +25,7 @@ IMAGE_TOKENS = WINDOW_ROWS * GROUP
 ROW_QUADS = 16
 SHIFT_TOKENS = GROUP // 2
 LN_EPS = 1e-5
+VECTOR_SLOTS = 1
 Z_BANKS = 3
 
 FLOPS = 2 * 2 * IMAGES * IMAGE_TOKENS * D * D
@@ -169,8 +170,9 @@ def tile_successiveswintransfomerblock_pb_t_kernel(tc, attn_win, x_mid, Wo2, bo2
             if not 0 <= g < GROUPS:
                 return
             x = resid.tile([P, QUAD, D], F32, name="x")
-            for q in range(QUAD):
-                nc.gpsimd.tensor_tensor(out=x[:, q, :], in0=live["xm_sb", g][:, q, :], in1=bo2_all[:], op=ADD)
+            nc.vector.tensor_tensor(
+                out=x[:], in0=live["xm_sb", g][:], in1=bo2_all[:].unsqueeze(1).to_broadcast([P, QUAD, D]), op=ADD
+            )
             live["x", g] = x
 
         def first_product(g):
@@ -227,11 +229,26 @@ def tile_successiveswintransfomerblock_pb_t_kernel(tc, attn_win, x_mid, Wo2, bo2
             live["rstd", g] = rstd
             live["shift", g] = shift
 
-        def normalise(g):
+        def normalise_on_vector(g):
             if not 0 <= g < GROUPS:
                 return
             z = work.tile([P, QUAD, D], F32, name="z")
-            for q in range(QUAD):
+            for q in range(QUAD - VECTOR_SLOTS, QUAD):
+                nc.vector.tensor_scalar(
+                    out=z[:, q, :],
+                    in0=live["x", g][:, q, :],
+                    scalar1=live["neg_mean", g][:, q : q + 1],
+                    scalar2=live["rstd", g][:, q : q + 1],
+                    op0=ADD,
+                    op1=MULT,
+                )
+            live["z", g] = z
+
+        def normalise(g):
+            if not 0 <= g < GROUPS:
+                return
+            z = live["z", g]
+            for q in range(QUAD - VECTOR_SLOTS):
                 nc.scalar.activation(
                     out=z[:, q, :],
                     in_=live["x", g][:, q, :],
@@ -239,7 +256,6 @@ def tile_successiveswintransfomerblock_pb_t_kernel(tc, attn_win, x_mid, Wo2, bo2
                     bias=live["shift", g][:, q : q + 1],
                     scale=live["rstd", g][:, q : q + 1],
                 )
-            live["z", g] = z
 
         def z_transpose(g, t):
             if not 0 <= g < GROUPS:
@@ -319,11 +335,12 @@ def tile_successiveswintransfomerblock_pb_t_kernel(tc, attn_win, x_mid, Wo2, bo2
             quantise_h(step - 2)
             add_bl(step - 1)
             variance(step)
-            add_bo2(step + 2)
             quantise_attn(step + 1)
+            normalise_on_vector(step)
             attn_copy_out(step + 2)
             second_product(step - 2)
             first_product(step + 1)
+            add_bo2(step + 2)
             normalise(step)
             regroup_h(step - 1)
             for t in range(Z_BANKS):

from contextlib import ExitStack

import concourse.mybir as mybir
from concourse.masks import make_identity

F32 = mybir.dt.float32
BF16 = mybir.dt.bfloat16
U32 = mybir.dt.uint32
U8 = mybir.dt.uint8
FP8X4 = mybir.dt.float8_e4m3fn_x4
ADD = mybir.AluOpType.add
MULT = mybir.AluOpType.mult
ACT = mybir.ActivationFunctionType

P = 128
D = 512
PACK = 4
QUAD = 4
GROUP = P * QUAD
IMAGES = 2
WINDOW_ROWS = 8
WS = 8
GROUPS = IMAGES * WINDOW_ROWS
IMAGE_TOKENS = WINDOW_ROWS * GROUP
ROW_QUADS = 16
SHIFT_TOKENS = GROUP // 2
LN_EPS = 1e-5
VECTOR_SLOTS = 1
Z_BANKS = 3

FLOPS = 2 * 2 * IMAGES * IMAGE_TOKENS * D * D


def quads(flat, first, count):
    return flat[first : first + count, :].rearrange("(p q) d -> p q d", q=QUAD)


def image_pieces(g):
    image, window_row = divmod(g, WINDOW_ROWS)
    base = image * IMAGE_TOKENS
    if window_row == 0:
        half = P // 2
        return [(0, half, base + IMAGE_TOKENS - SHIFT_TOKENS), (half, half, base)]
    return [(0, P, base + window_row * GROUP - SHIFT_TOKENS)]


def quantise_weight(nc, stage, keep, raw, label):
    grouped = stage.tile([P, D, PACK], BF16, name="grouped_" + label, align_bytes=64)
    nc.vector.tensor_copy(out=grouped[:], in_=raw[:].rearrange("p t n -> p n t"))
    codes = keep.tile([P, D], U32, name="codes_" + label, align_bytes=64)
    scales = keep.tile([P, D], U8, name="scales_" + label, align_bytes=64)
    nc.vector.quantize_mx(
        out=codes[:].bitcast(FP8X4), scales=scales[:], in_=grouped[:].rearrange("p n t -> p (n t)")
    )
    return codes, scales


def tile_successiveswintransfomerblock_pb_t_kernel(tc, attn_win, x_mid, Wo2, bo2, g4, b4, Wl, bl, out):
    nc = tc.nc
    attn_flat = attn_win.flatten_outer_dims()
    x_flat = x_mid.flatten_outer_dims()
    out_flat = out.flatten_outer_dims()

    with ExitStack() as ctx:
        keep = ctx.enter_context(tc.tile_pool(name="keep", bufs=1))
        stage = ctx.enter_context(tc.tile_pool(name="stage", bufs=1))
        loads = ctx.enter_context(tc.tile_pool(name="loads", bufs=3))
        work = ctx.enter_context(tc.tile_pool(name="work", bufs=2))
        resid = ctx.enter_context(tc.tile_pool(name="resid", bufs=6))
        stats = ctx.enter_context(tc.tile_pool(name="stats", bufs=4))
        psum_at = ctx.enter_context(tc.psum_pool(name="psum_at", bufs=2))
        psum_mm = ctx.enter_context(tc.psum_pool(name="psum_mm", bufs=3))
        psum_zt = ctx.enter_context(tc.psum_pool(name="psum_zt", bufs=Z_BANKS))
        ctx.enter_context(tc.manual_schedule())

        gb_rows = keep.tile([P, P], BF16, name="gb_rows")
        nc.vector.memset(gb_rows[:], 0.0)
        eps_col = keep.tile([P, 1], F32, name="eps_col")
        nc.vector.memset(eps_col[:], LN_EPS)

        wo_raw = stage.tile([P, PACK, D], BF16, name="wo_raw")
        for u in range(2):
            nc.sync.dma_start(
                out=wo_raw[:, 2 * u : 2 * u + 2, :],
                in_=Wo2[u * 2 * P : (u + 1) * 2 * P, :].rearrange("(p e) n -> p e n", e=2),
            )
        wl_raw = stage.tile([P, PACK, D], BF16, name="wl_raw")
        nc.sync.dma_start(out=wl_raw[:], in_=Wl.rearrange("(t p) n -> p t n", p=P))
        nc.scalar.dma_start(out=gb_rows[0:PACK, :], in_=g4.rearrange("(t p) -> t p", p=P))
        nc.scalar.dma_start(out=gb_rows[PACK : 2 * PACK, :], in_=b4.rearrange("(t p) -> t p", p=P))
        bo2_all = keep.tile([P, D], BF16, name="bo2_all")
        nc.scalar.dma_start(out=bo2_all[:], in_=bo2.partition_broadcast(P))
        bl_all = keep.tile([P, D], BF16, name="bl_all")
        nc.scalar.dma_start(out=bl_all[:], in_=bl.partition_broadcast(P))

        ident = keep.tile([P, P], F32, name="ident")
        make_identity(nc, ident[:])
        by_row = keep.tile([P, P], F32, name="by_row")
        nc.vector.tensor_copy(
            out=by_row[:].rearrange("p (r w h) -> p r w h", r=WS, w=WS),
            in_=ident[:].rearrange("p (w r h) -> p r w h", w=WS, r=WS),
        )
        to_image = keep.tile([P, P], F32, name="to_image")
        unrolled = by_row[:].rearrange("p (r m) -> p r m", m=ROW_QUADS)
        rolled = to_image[:].rearrange("p (r m) -> p r m", m=ROW_QUADS)
        nc.vector.tensor_copy(out=rolled[:, :, 0 : ROW_QUADS - 1], in_=unrolled[:, :, 1:ROW_QUADS])
        nc.vector.tensor_copy(out=rolled[:, :, ROW_QUADS - 1 : ROW_QUADS], in_=unrolled[:, :, 0:1])
        ident_bf = keep.tile([P, P], BF16, name="ident_bf")
        nc.vector.tensor_copy(out=ident_bf[:], in_=ident[:])

        wo_codes, wo_scales = quantise_weight(nc, stage, keep, wo_raw, "wo")
        wl_codes, wl_scales = quantise_weight(nc, stage, keep, wl_raw, "wl")

        gb_ps = psum_mm.tile([P, P], BF16, name="gb_ps", tag="acc")
        nc.tensor.transpose(gb_ps[:], gb_rows[:], ident_bf[:])
        gb_col = keep.tile([P, 2 * PACK], F32, name="gb_col")
        nc.vector.tensor_copy(out=gb_col[:], in_=gb_ps[:, 0 : 2 * PACK])

        live = {}

        def load(g):
            if not 0 <= g < GROUPS:
                return
            attn_sb = loads.tile([P, QUAD, D], BF16, name="attn_sb")
            nc.sync.dma_start(out=attn_sb[:], in_=quads(attn_flat, g * GROUP, GROUP))
            xm_sb = loads.tile([P, QUAD, D], BF16, name="xm_sb")
            for first_p, n_p, first_token in image_pieces(g):
                nc.sync.dma_start(out=xm_sb[first_p : first_p + n_p], in_=quads(x_flat, first_token, n_p * QUAD))
            live["attn_sb", g] = attn_sb
            live["xm_sb", g] = xm_sb

        def attn_transpose(g):
            if not 0 <= g < GROUPS:
                return
            attn_words = live["attn_sb", g][:].bitcast(F32)
            for pair in range(QUAD // 2):
                a_t = psum_at.tile([P, 2, 2, P], F32, name="a_t")
                for s in range(2):
                    for u in range(2):
                        nc.tensor.transpose(
                            a_t[:, s, u, :], attn_words[:, 2 * pair + s, u * P : (u + 1) * P], to_image[:]
                        )
                live["a_t", g, pair] = a_t

        def attn_copy_out(g):
            if not 0 <= g < GROUPS:
                return
            a_grouped = work.tile([P, QUAD, P, PACK], BF16, name="a_grouped", bufs=3, align_bytes=64)
            for pair in range(QUAD // 2):
                nc.scalar.copy(
                    out=a_grouped[:, 2 * pair : 2 * pair + 2].bitcast(F32),
                    in_=live["a_t", g, pair][:].rearrange("p s u r -> p s r u"),
                )
            live["a_grouped", g] = a_grouped

        def quantise_attn(g):
            if not 0 <= g < GROUPS:
                return
            a_codes = work.tile([P, GROUP], U32, name="a_codes", align_bytes=64)
            a_scales = work.tile([P, GROUP], U8, name="a_scales", align_bytes=64)
            nc.vector.quantize_mx(
                out=a_codes[:].bitcast(FP8X4),
                scales=a_scales[:],
                in_=live["a_grouped", g][:].rearrange("p q r t -> p (q r t)"),
            )
            live["a_codes", g] = a_codes
            live["a_scales", g] = a_scales

        def add_bo2(g):
            if not 0 <= g < GROUPS:
                return
            x = resid.tile([P, QUAD, D], F32, name="x")
            nc.vector.tensor_tensor(
                out=x[:], in0=live["xm_sb", g][:], in1=bo2_all[:].unsqueeze(1).to_broadcast([P, QUAD, D]), op=ADD
            )
            live["x", g] = x

        def first_product(g):
            if not 0 <= g < GROUPS:
                return
            x = live["x", g]
            x_sum = stats.tile([P, QUAD], F32, name="x_sum")
            for q in range(QUAD):
                tokens = slice(q * P, (q + 1) * P)
                acc1 = psum_mm.tile([P, D], F32, name="acc1", tag="acc")
                nc.tensor.matmul_mx(
                    out=acc1[:],
                    lhsT=live["a_codes", g][:, tokens].bitcast(FP8X4),
                    lhsT_scale=live["a_scales", g][:, tokens],
                    rhs=wo_codes[:].bitcast(FP8X4),
                    rhs_scale=wo_scales[:],
                    start=True,
                    stop=True,
                )
                nc.vector.scalar_tensor_tensor(
                    out=x[:, q, :],
                    in0=acc1[:],
                    scalar=1.0,
                    in1=x[:, q, :],
                    op0=MULT,
                    op1=ADD,
                    accum_out=x_sum[:, q : q + 1],
                )
            neg_mean = stats.tile([P, QUAD], F32, name="neg_mean")
            nc.gpsimd.tensor_scalar(out=neg_mean[:], in0=x_sum[:], scalar1=-1.0 / D, scalar2=0.0, op0=MULT, op1=ADD)
            live["neg_mean", g] = neg_mean

        def variance(g):
            if not 0 <= g < GROUPS:
                return
            neg_mean = live["neg_mean", g]
            sq_sum = stats.tile([P, QUAD], F32, name="sq_sum")
            for q in range(QUAD):
                squares = work.tile([P, D], BF16, name="squares")
                nc.scalar.activation(
                    out=squares[:],
                    in_=live["x", g][:, q, :],
                    func=ACT.Square,
                    bias=neg_mean[:, q : q + 1],
                    scale=1.0,
                    accum_out=sq_sum[:, q : q + 1],
                )
            rstd = stats.tile([P, QUAD], F32, name="rstd")
            nc.scalar.activation(
                out=rstd[:], in_=sq_sum[:], func=ACT.Abs_reciprocal_sqrt, bias=eps_col[:], scale=1.0 / D
            )
            shift = stats.tile([P, QUAD], F32, name="shift")
            nc.gpsimd.tensor_tensor(out=shift[:], in0=neg_mean[:], in1=rstd[:], op=MULT)
            live["rstd", g] = rstd
            live["shift", g] = shift

        def normalise_on_vector(g):
            if not 0 <= g < GROUPS:
                return
            z = work.tile([P, QUAD, D], F32, name="z")
            for q in range(QUAD - VECTOR_SLOTS, QUAD):
                nc.vector.tensor_scalar(
                    out=z[:, q, :],
                    in0=live["x", g][:, q, :],
                    scalar1=live["neg_mean", g][:, q : q + 1],
                    scalar2=live["rstd", g][:, q : q + 1],
                    op0=ADD,
                    op1=MULT,
                )
            live["z", g] = z

        def normalise(g):
            if not 0 <= g < GROUPS:
                return
            z = live["z", g]
            for q in range(QUAD - VECTOR_SLOTS):
                nc.scalar.activation(
                    out=z[:, q, :],
                    in_=live["x", g][:, q, :],
                    func=ACT.Identity,
                    bias=live["shift", g][:, q : q + 1],
                    scale=live["rstd", g][:, q : q + 1],
                )

        def z_transpose(g, t):
            if not 0 <= g < GROUPS:
                return
            z_t = psum_zt.tile([P, GROUP], F32, name="z_t")
            for q in range(QUAD):
                nc.tensor.transpose(z_t[:, q * P : (q + 1) * P], live["z", g][:, q, t * P : (t + 1) * P], ident[:])
            live["z_t", g, t] = z_t

        def gain_and_bias(g, t):
            if not 0 <= g < GROUPS:
                return
            if t == 0:
                live["h_t", g] = work.tile([P, PACK, GROUP], BF16, name="h_t")
            nc.scalar.activation(
                out=live["h_t", g][:, t, :],
                in_=live["z_t", g, t][:],
                func=ACT.Identity,
                bias=gb_col[:, PACK + t : PACK + t + 1],
                scale=gb_col[:, t : t + 1],
            )

        def regroup_h(g):
            if not 0 <= g < GROUPS:
                return
            h_grouped = work.tile([P, GROUP, PACK], BF16, name="h_grouped", align_bytes=64)
            nc.scalar.copy(
                out=h_grouped[:].rearrange("p (c i) t -> p c t i", i=4),
                in_=live["h_t", g][:].rearrange("p t (c i) -> p c t i", i=4),
            )
            live["h_grouped", g] = h_grouped

        def quantise_h(g):
            if not 0 <= g < GROUPS:
                return
            h_codes = work.tile([P, GROUP], U32, name="h_codes", align_bytes=64)
            h_scales = work.tile([P, GROUP], U8, name="h_scales", align_bytes=64)
            nc.vector.quantize_mx(
                out=h_codes[:].bitcast(FP8X4),
                scales=h_scales[:],
                in_=live["h_grouped", g][:].rearrange("p r t -> p (r t)"),
            )
            live["h_codes", g] = h_codes
            live["h_scales", g] = h_scales

        def add_bl(g):
            if not 0 <= g < GROUPS:
                return
            x = live["x", g]
            nc.vector.tensor_tensor(out=x[:], in0=x[:], in1=bl_all[:].unsqueeze(1).to_broadcast([P, QUAD, D]), op=ADD)

        def second_product(g):
            if not 0 <= g < GROUPS:
                return
            x = live["x", g]
            for q in range(QUAD):
                tokens = slice(q * P, (q + 1) * P)
                acc2 = psum_mm.tile([P, D], F32, name="acc2", tag="acc")
                nc.tensor.matmul_mx(
                    out=acc2[:],
                    lhsT=live["h_codes", g][:, tokens].bitcast(FP8X4),
                    lhsT_scale=live["h_scales", g][:, tokens],
                    rhs=wl_codes[:].bitcast(FP8X4),
                    rhs_scale=wl_scales[:],
                    start=True,
                    stop=True,
                )
                nc.vector.tensor_tensor(out=x[:, q, :], in0=acc2[:], in1=x[:, q, :], op=ADD)
                for first_p, n_p, first_token in image_pieces(g):
                    nc.sync.dma_start(
                        out=quads(out_flat, first_token, n_p * QUAD)[:, q, :], in_=x[first_p : first_p + n_p, q, :]
                    )

        for step in range(-3, GROUPS + 2):
            load(step + 3)
            attn_transpose(step + 2)
            quantise_h(step - 2)
            add_bl(step - 1)
            variance(step)
            quantise_attn(step + 1)
            normalise_on_vector(step)
            attn_copy_out(step + 2)
            second_product(step - 2)
            first_product(step + 1)
            add_bo2(step + 2)
            normalise(step)
            regroup_h(step - 1)
            for t in range(Z_BANKS):
                z_transpose(step, t)
            for t in range(PACK):
                gain_and_bias(step, t)
                if t + Z_BANKS < PACK:
                    z_transpose(step, t + Z_BANKS)
